import numpy as np
import ml_dtypes


def mxq(x, axis, fmt="e4m3"):
    dtype, down = {"e4m3": (ml_dtypes.float8_e4m3fn, 7), "e5m2": (ml_dtypes.float8_e5m2, 14)}[fmt]
    v = np.moveaxis(np.asarray(x, np.float32).astype(ml_dtypes.bfloat16).astype(np.float64), axis, -1)
    blocks = v.reshape(v.shape[:-1] + (-1, 32))
    amax = np.abs(blocks).max(-1, keepdims=True)
    byte = np.maximum(np.where(amax > 0, np.frexp(amax)[1] - 1 + 127, 0) - down, 1)
    scale = np.exp2(byte - 127.0)
    codes = (blocks / scale).astype(np.float32).astype(dtype).astype(np.float64)
    return np.moveaxis((codes * scale).reshape(v.shape), -1, axis)


WIDE = False


def mx_kscale(k):
    if not WIDE:
        return np.ones(k)
    levels = np.array([10, -10, 5, -5, 0])
    a = np.random.permutation(np.resize(levels, k // 512 * 4)).reshape(k // 512, 4)
    idx = np.arange(k)
    return np.exp2(a[idx // 512, idx % 128 // 32])


BF16 = ml_dtypes.bfloat16


def bf(x):
    return np.asarray(x, np.float32).astype(BF16)


def f64(x):
    return np.asarray(x).astype(np.float64)


B, N, DIM, HEADS, DIM_HEAD = 2, 64, 512, 16, 64
INNER = HEADS * DIM_HEAD


def setup_inputs():
    s = mx_kscale(DIM)
    return {"x": bf(np.random.standard_normal((B, N, DIM)) * s),
            "W": bf(np.random.standard_normal((3 * INNER, DIM)) / np.sqrt(DIM) / s[None, :])}


def reference(x, W):
    b, n, _ = x.shape
    qkv = mxq(f64(x), 2, "e4m3") @ mxq(f64(W), 1, "e4m3").T
    q, k, v = np.split(qkv, 3, axis=-1)

    def to_heads(t):
        return t.reshape(b, n, HEADS, DIM_HEAD).transpose(0, 2, 1, 3)

    return to_heads(q), to_heads(k), to_heads(v)

@@ -1,0 +1,133 @@
+from contextlib import ExitStack
+
+import concourse.mybir as mybir
+from concourse.masks import make_identity
+
+BF16 = mybir.dt.bfloat16
+F32 = mybir.dt.float32
+U32 = mybir.dt.uint32
+U8 = mybir.dt.uint8
+FP8X4 = mybir.dt.float8_e4m3fn_x4
+
+P = 128
+PACK = 4
+BATCH, TOKENS, DIM = 2, 64, 512
+HEADS, DIM_HEAD = 16, 64
+PARTS = 3
+WORDS = DIM // 2
+HALVES = WORDS // P
+CHUNK = 512
+ROWS = CHUNK // P
+CHUNKS = PARTS * HEADS * DIM_HEAD // CHUNK
+CHUNKS_PER_PART = HEADS * DIM_HEAD // CHUNK
+CHUNK_HEADS = CHUNK // DIM_HEAD
+BANK_ROWS = 2
+
+FLOPS = 2 * BATCH * TOKENS * DIM * PARTS * HEADS * DIM_HEAD
+
+
+def tile_get_qkv_s_kernel(tc, x, W, out_0, out_1, out_2):
+    nc = tc.nc
+    outs = [out_0, out_1, out_2]
+
+    with ExitStack() as ctx:
+        keep = ctx.enter_context(tc.tile_pool(name="keep", bufs=1))
+        stage = ctx.enter_context(tc.tile_pool(name="stage", bufs=3))
+        psum_x = ctx.enter_context(tc.psum_pool(name="psum_x", bufs=1))
+        psum_w = ctx.enter_context(tc.psum_pool(name="psum_w", bufs=4))
+        psum_acc = ctx.enter_context(tc.psum_pool(name="psum_acc", bufs=3))
+        ctx.enter_context(tc.manual_schedule())
+
+        x_raw = keep.tile([P, DIM], BF16)
+        nc.sync.dma_start(out=x_raw[:], in_=x.rearrange("b n d -> (b n) d"))
+        w_raw = []
+        for c in range(CHUNKS):
+            raw = keep.tile([P, ROWS * DIM], BF16, name="w_raw%d" % c)
+            nc.sync.dma_start(
+                out=raw[:],
+                in_=W[c * CHUNK : (c + 1) * CHUNK, :].rearrange("(p r) d -> p (r d)", r=ROWS),
+            )
+            w_raw.append(raw)
+
+        ident = keep.tile([P, P], F32)
+        make_identity(nc, ident[:])
+
+        x_codes = keep.tile([P, P], U32, align_bytes=64)
+        x_scales = keep.tile([P, P], U8, align_bytes=64)
+        w_codes = keep.tile([P, CHUNKS, CHUNK], U32, align_bytes=64)
+        w_scales = keep.tile([P, CHUNKS, CHUNK], U8, align_bytes=64)
+
+        def transpose_x():
+            x_words = x_raw[:].bitcast(F32)
+            turned = psum_x.tile([P, HALVES, P], F32)
+            for half in range(HALVES):
+                nc.tensor.transpose(turned[:, half, :], x_words[:, half * P : (half + 1) * P], ident[:])
+            grouped = stage.tile([P, P * PACK], BF16, name="x_grouped", align_bytes=64)
+            nc.scalar.copy(
+                out=grouped[:].bitcast(F32).rearrange("q (m h) -> q m h", h=HALVES),
+                in_=turned[:].rearrange("q h m -> q m h"),
+            )
+            return grouped
+
+        def transpose_chunk(c):
+            w_words = w_raw[c][:].bitcast(F32)
+            grouped = stage.tile([P, CHUNK * PACK], BF16, name="w_grouped", align_bytes=64)
+            grouped_words = grouped[:].bitcast(F32)
+            bank_words = BANK_ROWS * P * HALVES
+            for bank in range(ROWS // BANK_ROWS):
+                turned = psum_w.tile([P, BANK_ROWS, HALVES, P], F32)
+                for r in range(BANK_ROWS):
+                    for half in range(HALVES):
+                        first = (bank * BANK_ROWS + r) * WORDS + half * P
+                        nc.tensor.transpose(turned[:, r, half, :], w_words[:, first : first + P], ident[:])
+                nc.scalar.copy(
+                    out=grouped_words[:, bank * bank_words : (bank + 1) * bank_words].rearrange(
+                        "q (r p h) -> q r p h", r=BANK_ROWS, h=HALVES
+                    ),
+                    in_=turned[:].rearrange("q r h p -> q r p h"),
+                )
+            return grouped
+
+        def multiply_chunk(c):
+            acc = psum_acc.tile([P, CHUNK], F32)
+            nc.tensor.matmul_mx(
+                out=acc[:],
+                lhsT=x_codes[:].bitcast(FP8X4),
+                lhsT_scale=x_scales[:],
+                rhs=w_codes[:, c, :].bitcast(FP8X4),
+                rhs_scale=w_scales[:, c, :],
+                start=True,
+                stop=True,
+            )
+            return acc
+
+        def store_chunk(c, acc):
+            result = keep.tile([P, CHUNK], F32, name="result%d" % c)
+            nc.vector.tensor_copy(
+                out=result[:].rearrange("m (p r) -> m p r", r=ROWS),
+                in_=acc[:].rearrange("m (r p) -> m p r", r=ROWS),
+            )
+            part = outs[c // CHUNKS_PER_PART]
+            head = (c % CHUNKS_PER_PART) * CHUNK_HEADS
+            for b in range(BATCH):
+                nc.sync.dma_start(
+                    out=part[b, head : head + CHUNK_HEADS, :, :].rearrange("h n d -> n h d"),
+                    in_=result[b * TOKENS : (b + 1) * TOKENS, :].rearrange("n (h d) -> n h d", d=DIM_HEAD),
+                )
+
+        x_grouped = transpose_x()
+        grouped_next = transpose_chunk(0)
+        nc.vector.quantize_mx(out=x_codes[:].bitcast(FP8X4), scales=x_scales[:], in_=x_grouped[:])
+        acc_before = None
+        for c in range(CHUNKS):
+            grouped_now = grouped_next
+            if c + 1 < CHUNKS:
+                grouped_next = transpose_chunk(c + 1)
+            nc.vector.quantize_mx(
+                out=w_codes[:, c, :].bitcast(FP8X4), scales=w_scales[:, c, :], in_=grouped_now[:]
+            )
+            acc_now = multiply_chunk(c)
+            if c > 0:
+                store_chunk(c - 1, acc_before)
+            acc_before = acc_now
+        store_chunk(CHUNKS - 1, acc_before)

@@ -39,7 +39,8 @@ def tile_get_qkv_s_kernel(tc, x, W, out_0, out_1, out_2):
         ctx.enter_context(tc.manual_schedule())
 
         x_raw = keep.tile([P, DIM], BF16)
-        nc.sync.dma_start(out=x_raw[:], in_=x.rearrange("b n d -> (b n) d"))
+        for b in range(BATCH):
+            nc.sync.dma_start(out=x_raw[b:P:BATCH, :], in_=x[b, :, :])
         w_raw = []
         for c in range(CHUNKS):
             raw = keep.tile([P, ROWS * DIM], BF16, name="w_raw%d" % c)
@@ -112,7 +113,7 @@ def tile_get_qkv_s_kernel(tc, x, W, out_0, out_1, out_2):
             for b in range(BATCH):
                 nc.sync.dma_start(
                     out=part[b, head : head + CHUNK_HEADS, :, :].rearrange("h n d -> n h d"),
-                    in_=result[b * TOKENS : (b + 1) * TOKENS, :].rearrange("n (h d) -> n h d", d=DIM_HEAD),
+                    in_=result[b:P:BATCH, :].rearrange("n (h d) -> n h d", d=DIM_HEAD),
                 )
 
         x_grouped = transpose_x()

@@ -23,6 +23,10 @@ CHUNKS_PER_PART = HEADS * DIM_HEAD // CHUNK
 CHUNK_HEADS = CHUNK // DIM_HEAD
 BANK_ROWS = 2
 
+QUANTISE_LAG, MULTIPLY_LAG, STORE_LAG = 1, 2, 3
+WARM_PASSES = 16
+FILL_PASSES = CHUNK // P
+
 FLOPS = 2 * BATCH * TOKENS * DIM * PARTS * HEADS * DIM_HEAD
 
 
@@ -58,6 +62,38 @@ def tile_get_qkv_s_kernel(tc, x, W, out_0, out_1, out_2):
         w_codes = keep.tile([P, CHUNKS, CHUNK], U32, align_bytes=64)
         w_scales = keep.tile([P, CHUNKS, CHUNK], U8, align_bytes=64)
 
+        zeros = keep.tile([P, P * PACK], BF16, align_bytes=64)
+        zero_codes = keep.tile([P, P], U32, align_bytes=64)
+        zero_scales = keep.tile([P, P], U8, align_bytes=64)
+        nc.vector.memset(zeros[:], 0.0)
+        nc.vector.quantize_mx(out=zero_codes[:].bitcast(FP8X4), scales=zero_scales[:], in_=zeros[:])
+
+        def keep_tensor_engine_busy(passes):
+            unread = psum_acc.tile([P, CHUNK], F32, tag="acc")
+            for i in range(passes):
+                nc.tensor.matmul_mx(
+                    out=unread[:, :P],
+                    lhsT=zero_codes[:].bitcast(FP8X4),
+                    lhsT_scale=zero_scales[:],
+                    rhs=zero_codes[:].bitcast(FP8X4),
+                    rhs_scale=zero_scales[:],
+                    start=True,
+                    stop=True,
+                )
+
+        def multiply_chunk(c):
+            acc = psum_acc.tile([P, CHUNK], F32, tag="acc")
+            nc.tensor.matmul_mx(
+                out=acc[:],
+                lhsT=x_codes[:].bitcast(FP8X4),
+                lhsT_scale=x_scales[:],
+                rhs=w_codes[:, c, :].bitcast(FP8X4),
+                rhs_scale=w_scales[:, c, :],
+                start=True,
+                stop=True,
+            )
+            return acc
+
         def transpose_x():
             x_words = x_raw[:].bitcast(F32)
             turned = psum_x.tile([P, HALVES, P], F32)
@@ -89,19 +125,6 @@ def tile_get_qkv_s_kernel(tc, x, W, out_0, out_1, out_2):
                 )
             return grouped
 
-        def multiply_chunk(c):
-            acc = psum_acc.tile([P, CHUNK], F32)
-            nc.tensor.matmul_mx(
-                out=acc[:],
-                lhsT=x_codes[:].bitcast(FP8X4),
-                lhsT_scale=x_scales[:],
-                rhs=w_codes[:, c, :].bitcast(FP8X4),
-                rhs_scale=w_scales[:, c, :],
-                start=True,
-                stop=True,
-            )
-            return acc
-
         def store_chunk(c, acc):
             result = keep.tile([P, CHUNK], F32, name="result%d" % c)
             nc.vector.tensor_copy(
@@ -116,19 +139,28 @@ def tile_get_qkv_s_kernel(tc, x, W, out_0, out_1, out_2):
                     in_=result[b:P:BATCH, :].rearrange("n (h d) -> n h d", d=DIM_HEAD),
                 )
 
+        keep_tensor_engine_busy(WARM_PASSES)
         x_grouped = transpose_x()
-        grouped_next = transpose_chunk(0)
         nc.vector.quantize_mx(out=x_codes[:].bitcast(FP8X4), scales=x_scales[:], in_=x_grouped[:])
-        acc_before = None
-        for c in range(CHUNKS):
-            grouped_now = grouped_next
-            if c + 1 < CHUNKS:
-                grouped_next = transpose_chunk(c + 1)
-            nc.vector.quantize_mx(
-                out=w_codes[:, c, :].bitcast(FP8X4), scales=w_scales[:, c, :], in_=grouped_now[:]
-            )
-            acc_now = multiply_chunk(c)
-            if c > 0:
-                store_chunk(c - 1, acc_before)
-            acc_before = acc_now
-        store_chunk(CHUNKS - 1, acc_before)
+
+        grouped = {}
+        acc = {}
+        for step in range(CHUNKS + STORE_LAG):
+            if step < CHUNKS:
+                grouped[step] = transpose_chunk(step)
+
+            c = step - STORE_LAG
+            if c >= 0:
+                store_chunk(c, acc[c])
+
+            c = step - QUANTISE_LAG
+            if 0 <= c < CHUNKS:
+                nc.vector.quantize_mx(
+                    out=w_codes[:, c, :].bitcast(FP8X4), scales=w_scales[:, c, :], in_=grouped[c][:]
+                )
+
+            c = step - MULTIPLY_LAG
+            if c < 0:
+                keep_tensor_engine_busy(FILL_PASSES)
+            elif c < CHUNKS:
+                acc[c] = multiply_chunk(c)

@@ -24,8 +24,6 @@ CHUNK_HEADS = CHUNK // DIM_HEAD
 BANK_ROWS = 2
 
 QUANTISE_LAG, MULTIPLY_LAG, STORE_LAG = 1, 2, 3
-WARM_PASSES = 16
-FILL_PASSES = CHUNK // P
 
 FLOPS = 2 * BATCH * TOKENS * DIM * PARTS * HEADS * DIM_HEAD
 
@@ -62,27 +60,8 @@ def tile_get_qkv_s_kernel(tc, x, W, out_0, out_1, out_2):
         w_codes = keep.tile([P, CHUNKS, CHUNK], U32, align_bytes=64)
         w_scales = keep.tile([P, CHUNKS, CHUNK], U8, align_bytes=64)
 
-        zeros = keep.tile([P, P * PACK], BF16, align_bytes=64)
-        zero_codes = keep.tile([P, P], U32, align_bytes=64)
-        zero_scales = keep.tile([P, P], U8, align_bytes=64)
-        nc.vector.memset(zeros[:], 0.0)
-        nc.vector.quantize_mx(out=zero_codes[:].bitcast(FP8X4), scales=zero_scales[:], in_=zeros[:])
-
-        def keep_tensor_engine_busy(passes):
-            unread = psum_acc.tile([P, CHUNK], F32, tag="acc")
-            for i in range(passes):
-                nc.tensor.matmul_mx(
-                    out=unread[:, :P],
-                    lhsT=zero_codes[:].bitcast(FP8X4),
-                    lhsT_scale=zero_scales[:],
-                    rhs=zero_codes[:].bitcast(FP8X4),
-                    rhs_scale=zero_scales[:],
-                    start=True,
-                    stop=True,
-                )
-
         def multiply_chunk(c):
-            acc = psum_acc.tile([P, CHUNK], F32, tag="acc")
+            acc = psum_acc.tile([P, CHUNK], F32)
             nc.tensor.matmul_mx(
                 out=acc[:],
                 lhsT=x_codes[:].bitcast(FP8X4),
@@ -139,7 +118,6 @@ def tile_get_qkv_s_kernel(tc, x, W, out_0, out_1, out_2):
                     in_=result[b:P:BATCH, :].rearrange("n (h d) -> n h d", d=DIM_HEAD),
                 )
 
-        keep_tensor_engine_busy(WARM_PASSES)
         x_grouped = transpose_x()
         nc.vector.quantize_mx(out=x_codes[:].bitcast(FP8X4), scales=x_scales[:], in_=x_grouped[:])
 
@@ -160,7 +138,5 @@ def tile_get_qkv_s_kernel(tc, x, W, out_0, out_1, out_2):
                 )
 
             c = step - MULTIPLY_LAG
-            if c < 0:
-                keep_tensor_engine_busy(FILL_PASSES)
-            elif c < CHUNKS:
+            if 0 <= c < CHUNKS:
                 acc[c] = multiply_chunk(c)

@@ -22,6 +22,7 @@ CHUNKS = PARTS * HEADS * DIM_HEAD // CHUNK
 CHUNKS_PER_PART = HEADS * DIM_HEAD // CHUNK
 CHUNK_HEADS = CHUNK // DIM_HEAD
 BANK_ROWS = 2
+CHUNK_BANKS = ROWS // BANK_ROWS
 
 QUANTISE_LAG, MULTIPLY_LAG, STORE_LAG = 1, 2, 3
 
@@ -36,7 +37,7 @@ def tile_get_qkv_s_kernel(tc, x, W, out_0, out_1, out_2):
         keep = ctx.enter_context(tc.tile_pool(name="keep", bufs=1))
         stage = ctx.enter_context(tc.tile_pool(name="stage", bufs=3))
         psum_x = ctx.enter_context(tc.psum_pool(name="psum_x", bufs=1))
-        psum_w = ctx.enter_context(tc.psum_pool(name="psum_w", bufs=4))
+        psum_w = ctx.enter_context(tc.psum_pool(name="psum_w", bufs=2 * CHUNK_BANKS))
         psum_acc = ctx.enter_context(tc.psum_pool(name="psum_acc", bufs=3))
         ctx.enter_context(tc.manual_schedule())
 
@@ -60,25 +61,12 @@ def tile_get_qkv_s_kernel(tc, x, W, out_0, out_1, out_2):
         w_codes = keep.tile([P, CHUNKS, CHUNK], U32, align_bytes=64)
         w_scales = keep.tile([P, CHUNKS, CHUNK], U8, align_bytes=64)
 
-        def multiply_chunk(c):
-            acc = psum_acc.tile([P, CHUNK], F32)
-            nc.tensor.matmul_mx(
-                out=acc[:],
-                lhsT=x_codes[:].bitcast(FP8X4),
-                lhsT_scale=x_scales[:],
-                rhs=w_codes[:, c, :].bitcast(FP8X4),
-                rhs_scale=w_scales[:, c, :],
-                start=True,
-                stop=True,
-            )
-            return acc
-
         def transpose_x():
             x_words = x_raw[:].bitcast(F32)
             turned = psum_x.tile([P, HALVES, P], F32)
             for half in range(HALVES):
                 nc.tensor.transpose(turned[:, half, :], x_words[:, half * P : (half + 1) * P], ident[:])
-            grouped = stage.tile([P, P * PACK], BF16, name="x_grouped", align_bytes=64)
+            grouped = keep.tile([P, P * PACK], BF16, name="x_grouped", align_bytes=64)
             nc.scalar.copy(
                 out=grouped[:].bitcast(F32).rearrange("q (m h) -> q m h", h=HALVES),
                 in_=turned[:].rearrange("q h m -> q m h"),
@@ -90,7 +78,7 @@ def tile_get_qkv_s_kernel(tc, x, W, out_0, out_1, out_2):
             grouped = stage.tile([P, CHUNK * PACK], BF16, name="w_grouped", align_bytes=64)
             grouped_words = grouped[:].bitcast(F32)
             bank_words = BANK_ROWS * P * HALVES
-            for bank in range(ROWS // BANK_ROWS):
+            for bank in range(CHUNK_BANKS):
                 turned = psum_w.tile([P, BANK_ROWS, HALVES, P], F32)
                 for r in range(BANK_ROWS):
                     for half in range(HALVES):
@@ -104,9 +92,22 @@ def tile_get_qkv_s_kernel(tc, x, W, out_0, out_1, out_2):
                 )
             return grouped
 
-        def store_chunk(c, acc):
+        def multiply_chunk(c):
+            acc = psum_acc.tile([P, CHUNK], F32)
+            nc.tensor.matmul_mx(
+                out=acc[:],
+                lhsT=x_codes[:].bitcast(FP8X4),
+                lhsT_scale=x_scales[:],
+                rhs=w_codes[:, c, :].bitcast(FP8X4),
+                rhs_scale=w_scales[:, c, :],
+                start=True,
+                stop=True,
+            )
+            return acc
+
+        def store_chunk(c, acc, copy_out):
             result = keep.tile([P, CHUNK], F32, name="result%d" % c)
-            nc.vector.tensor_copy(
+            copy_out(
                 out=result[:].rearrange("m (p r) -> m p r", r=ROWS),
                 in_=acc[:].rearrange("m (r p) -> m p r", r=ROWS),
             )
@@ -121,22 +122,22 @@ def tile_get_qkv_s_kernel(tc, x, W, out_0, out_1, out_2):
         x_grouped = transpose_x()
         nc.vector.quantize_mx(out=x_codes[:].bitcast(FP8X4), scales=x_scales[:], in_=x_grouped[:])
 
-        grouped = {}
-        acc = {}
+        grouped_of = {}
+        acc_of = {}
         for step in range(CHUNKS + STORE_LAG):
             if step < CHUNKS:
-                grouped[step] = transpose_chunk(step)
+                grouped_of[step] = transpose_chunk(step)
 
             c = step - STORE_LAG
             if c >= 0:
-                store_chunk(c, acc[c])
+                store_chunk(c, acc_of[c], nc.vector.tensor_copy if step < CHUNKS else nc.scalar.copy)
 
             c = step - QUANTISE_LAG
             if 0 <= c < CHUNKS:
                 nc.vector.quantize_mx(
-                    out=w_codes[:, c, :].bitcast(FP8X4), scales=w_scales[:, c, :], in_=grouped[c][:]
+                    out=w_codes[:, c, :].bitcast(FP8X4), scales=w_scales[:, c, :], in_=grouped_of[c][:]
                 )
 
             c = step - MULTIPLY_LAG
             if 0 <= c < CHUNKS:
-                acc[c] = multiply_chunk(c)
+                acc_of[c] = multiply_chunk(c)

from contextlib import ExitStack

import concourse.mybir as mybir
from concourse.masks import make_identity

BF16 = mybir.dt.bfloat16
F32 = mybir.dt.float32
U32 = mybir.dt.uint32
U8 = mybir.dt.uint8
FP8X4 = mybir.dt.float8_e4m3fn_x4

P = 128
PACK = 4
BATCH, TOKENS, DIM = 2, 64, 512
HEADS, DIM_HEAD = 16, 64
PARTS = 3
WORDS = DIM // 2
HALVES = WORDS // P
CHUNK = 512
ROWS = CHUNK // P
CHUNKS = PARTS * HEADS * DIM_HEAD // CHUNK
CHUNKS_PER_PART = HEADS * DIM_HEAD // CHUNK
CHUNK_HEADS = CHUNK // DIM_HEAD
BANK_ROWS = 2
CHUNK_BANKS = ROWS // BANK_ROWS

QUANTISE_LAG, MULTIPLY_LAG, STORE_LAG = 1, 2, 3

FLOPS = 2 * BATCH * TOKENS * DIM * PARTS * HEADS * DIM_HEAD


def tile_get_qkv_s_kernel(tc, x, W, out_0, out_1, out_2):
    nc = tc.nc
    outs = [out_0, out_1, out_2]

    with ExitStack() as ctx:
        keep = ctx.enter_context(tc.tile_pool(name="keep", bufs=1))
        stage = ctx.enter_context(tc.tile_pool(name="stage", bufs=3))
        psum_x = ctx.enter_context(tc.psum_pool(name="psum_x", bufs=1))
        psum_w = ctx.enter_context(tc.psum_pool(name="psum_w", bufs=2 * CHUNK_BANKS))
        psum_acc = ctx.enter_context(tc.psum_pool(name="psum_acc", bufs=3))
        ctx.enter_context(tc.manual_schedule())

        x_raw = keep.tile([P, DIM], BF16)
        for b in range(BATCH):
            nc.sync.dma_start(out=x_raw[b:P:BATCH, :], in_=x[b, :, :])
        w_raw = []
        for c in range(CHUNKS):
            raw = keep.tile([P, ROWS * DIM], BF16, name="w_raw%d" % c)
            nc.sync.dma_start(
                out=raw[:],
                in_=W[c * CHUNK : (c + 1) * CHUNK, :].rearrange("(p r) d -> p (r d)", r=ROWS),
            )
            w_raw.append(raw)

        ident = keep.tile([P, P], F32)
        make_identity(nc, ident[:])

        x_codes = keep.tile([P, P], U32, align_bytes=64)
        x_scales = keep.tile([P, P], U8, align_bytes=64)
        w_codes = keep.tile([P, CHUNKS, CHUNK], U32, align_bytes=64)
        w_scales = keep.tile([P, CHUNKS, CHUNK], U8, align_bytes=64)

        def transpose_x():
            x_words = x_raw[:].bitcast(F32)
            turned = psum_x.tile([P, HALVES, P], F32)
            for half in range(HALVES):
                nc.tensor.transpose(turned[:, half, :], x_words[:, half * P : (half + 1) * P], ident[:])
            grouped = keep.tile([P, P * PACK], BF16, name="x_grouped", align_bytes=64)
            nc.scalar.copy(
                out=grouped[:].bitcast(F32).rearrange("q (m h) -> q m h", h=HALVES),
                in_=turned[:].rearrange("q h m -> q m h"),
            )
            return grouped

        def transpose_chunk(c):
            w_words = w_raw[c][:].bitcast(F32)
            grouped = stage.tile([P, CHUNK * PACK], BF16, name="w_grouped", align_bytes=64)
            grouped_words = grouped[:].bitcast(F32)
            bank_words = BANK_ROWS * P * HALVES
            for bank in range(CHUNK_BANKS):
                turned = psum_w.tile([P, BANK_ROWS, HALVES, P], F32)
                for r in range(BANK_ROWS):
                    for half in range(HALVES):
                        first = (bank * BANK_ROWS + r) * WORDS + half * P
                        nc.tensor.transpose(turned[:, r, half, :], w_words[:, first : first + P], ident[:])
                nc.scalar.copy(
                    out=grouped_words[:, bank * bank_words : (bank + 1) * bank_words].rearrange(
                        "q (r p h) -> q r p h", r=BANK_ROWS, h=HALVES
                    ),
                    in_=turned[:].rearrange("q r h p -> q r p h"),
                )
            return grouped

        def multiply_chunk(c):
            acc = psum_acc.tile([P, CHUNK], F32)
            nc.tensor.matmul_mx(
                out=acc[:],
                lhsT=x_codes[:].bitcast(FP8X4),
                lhsT_scale=x_scales[:],
                rhs=w_codes[:, c, :].bitcast(FP8X4),
                rhs_scale=w_scales[:, c, :],
                start=True,
                stop=True,
            )
            return acc

        def store_chunk(c, acc, copy_out):
            result = keep.tile([P, CHUNK], F32, name="result%d" % c)
            copy_out(
                out=result[:].rearrange("m (p r) -> m p r", r=ROWS),
                in_=acc[:].rearrange("m (r p) -> m p r", r=ROWS),
            )
            part = outs[c // CHUNKS_PER_PART]
            head = (c % CHUNKS_PER_PART) * CHUNK_HEADS
            for b in range(BATCH):
                nc.sync.dma_start(
                    out=part[b, head : head + CHUNK_HEADS, :, :].rearrange("h n d -> n h d"),
                    in_=result[b:P:BATCH, :].rearrange("n (h d) -> n h d", d=DIM_HEAD),
                )

        x_grouped = transpose_x()
        nc.vector.quantize_mx(out=x_codes[:].bitcast(FP8X4), scales=x_scales[:], in_=x_grouped[:])

        grouped_of = {}
        acc_of = {}
        for step in range(CHUNKS + STORE_LAG):
            if step < CHUNKS:
                grouped_of[step] = transpose_chunk(step)

            c = step - STORE_LAG
            if c >= 0:
                store_chunk(c, acc_of[c], nc.vector.tensor_copy if step < CHUNKS else nc.scalar.copy)

            c = step - QUANTISE_LAG
            if 0 <= c < CHUNKS:
                nc.vector.quantize_mx(
                    out=w_codes[:, c, :].bitcast(FP8X4), scales=w_scales[:, c, :], in_=grouped_of[c][:]
                )

            c = step - MULTIPLY_LAG
            if 0 <= c < CHUNKS:
                acc_of[c] = multiply_chunk(c)
